import numpy as np
import ml_dtypes


def mxq(x, axis, fmt="e4m3"):
    dtype, down = {"e4m3": (ml_dtypes.float8_e4m3fn, 7), "e5m2": (ml_dtypes.float8_e5m2, 14)}[fmt]
    v = np.moveaxis(np.asarray(x, np.float32).astype(ml_dtypes.bfloat16).astype(np.float64), axis, -1)
    blocks = v.reshape(v.shape[:-1] + (-1, 32))
    amax = np.abs(blocks).max(-1, keepdims=True)
    byte = np.maximum(np.where(amax > 0, np.frexp(amax)[1] - 1 + 127, 0) - down, 1)
    scale = np.exp2(byte - 127.0)
    codes = (blocks / scale).astype(np.float32).astype(dtype).astype(np.float64)
    return np.moveaxis((codes * scale).reshape(v.shape), -1, axis)


WIDE = False


def mx_kscale(k):
    if not WIDE:
        return np.ones(k)
    levels = np.array([10, -10, 5, -5, 0])
    a = np.random.permutation(np.resize(levels, k // 512 * 4)).reshape(k // 512, 4)
    idx = np.arange(k)
    return np.exp2(a[idx // 512, idx % 128 // 32])


BF16 = ml_dtypes.bfloat16


def bf(x):
    return np.asarray(x, np.float32).astype(BF16)


def f64(x):
    return np.asarray(x).astype(np.float64)


S, D, H, DH, F = 8192, 1024, 1, 128, 4096
E = H * DH
EPS = 1e-5
XS = 0.015


def fixed_pos_embedding(seq_len, dim):
    inv_freq = 1.0 / (10000.0 ** (np.arange(0, dim, 2) / dim))
    sinusoid = np.arange(seq_len, dtype=np.float64)[:, None] * inv_freq[None, :]
    sin = np.concatenate([np.sin(sinusoid)] * 2, axis=-1)[:, :dim]
    cos = np.concatenate([np.cos(sinusoid)] * 2, axis=-1)[:, :dim]
    return sin, cos


def rotate_every_two(y):
    return np.stack((-y[..., 1::2], y[..., ::2]), axis=-1).reshape(y.shape)


def apply_rotary(y, sin, cos):
    return rotate_every_two(y) * sin[:, None, :] + y * cos[:, None, :]


def layernorm(x, scale, offset):
    mean = x.mean(axis=-1, keepdims=True)
    var = x.var(axis=-1, keepdims=True)
    return scale / np.sqrt(var + EPS) * (x - mean) + offset


def setup_inputs():
    s = mx_kscale(D)
    x = np.random.standard_normal((S, D)) + 0.5 * np.random.standard_normal(S)[:, None]
    return {"x": bf(XS * x[None]),
            "ln_scale": bf((1.0 + 0.1 * np.random.standard_normal(D)) * s),
            "ln_offset": bf(0.1 * np.random.standard_normal(D) * s),
            "Wq": bf(np.random.standard_normal((D, E)) * 0.7 / np.sqrt(D) / s[:, None]),
            "Wk": bf(np.random.standard_normal((D, E)) * 0.7 / np.sqrt(D) / s[:, None]),
            "Wv": bf(np.random.standard_normal((D, E)) / np.sqrt(D) / s[:, None])}


def reference(x, ln_scale, ln_offset, Wq, Wk, Wv):
    x = f64(x)
    b, s, _ = x.shape
    xn = layernorm(x, f64(ln_scale), f64(ln_offset))
    xq = mxq(xn, 2, "e4m3")

    def proj(W):
        h = (xq @ mxq(f64(W), 0, "e4m3")).reshape(b, s, H, DH)
        return np.transpose(h, (1, 0, 2, 3)).reshape(s, b * H, DH)

    q, v, k = proj(Wq), proj(Wv), proj(Wk)
    sin, cos = fixed_pos_embedding(s, DH)
    return apply_rotary(q, sin, cos), apply_rotary(k, sin, cos), v

@@ -1,0 +1,301 @@
+import math
+from contextlib import ExitStack
+
+import concourse.mybir as mybir
+from concourse.masks import make_identity
+
+F32 = mybir.dt.float32
+BF16 = mybir.dt.bfloat16
+I32 = mybir.dt.int32
+U32 = mybir.dt.uint32
+U8 = mybir.dt.uint8
+FP8X4 = mybir.dt.float8_e4m3fn_x4
+ALU = mybir.AluOpType
+ACT = mybir.ActivationFunctionType
+
+P = 128
+S = 8192
+D = 1024
+DH = 128
+EPS = 1e-5
+PACK = 4
+CHUNKS = D // P
+PASSES = D // (P * PACK)
+TILES = S // P
+GROUP = 4
+GROUPS = TILES // GROUP
+BANK = 512
+FREQS = DH // 2
+ROUND_MAGIC = 12582912.0
+HI_GRID = 2.0 ** 19
+
+FLOPS = 2 * S * D * 3 * DH
+
+
+def load_layer_norm_columns(nc, setup, keep, banks, ident, ln_scale, ln_offset):
+    rows = setup.tile([P, P], BF16, name="gb_rows")
+    nc.vector.memset(rows[:], 0.0)
+    nc.sync.dma_start(out=rows[0:CHUNKS, :], in_=ln_scale.rearrange("(c p) -> c p", p=P))
+    nc.sync.dma_start(
+        out=rows[CHUNKS : 2 * CHUNKS, :], in_=ln_offset.rearrange("(c p) -> c p", p=P)
+    )
+    rows32 = setup.tile([P, P], F32, name="gb_rows32")
+    nc.vector.tensor_copy(out=rows32[:], in_=rows[:])
+    turned = banks.tile([P, BANK], F32, tag="turned")
+    nc.tensor.transpose(turned[:, 0:P], rows32[:], ident[:])
+    gain_bias = keep.tile([P, 2 * CHUNKS], F32, name="gain_bias")
+    nc.vector.tensor_copy(out=gain_bias[:], in_=turned[:, 0 : 2 * CHUNKS])
+    return gain_bias
+
+
+def quantise_weights(nc, setup, keep, Wq, Wk, Wv):
+    qk_grouped = setup.tile([P, PASSES, BANK, PACK], BF16, name="qk_grouped", align_bytes=64)
+    v_grouped = setup.tile([P, PASSES, DH, PACK], BF16, name="v_grouped", align_bytes=64)
+    for g, w in enumerate((Wq, Wk)):
+        raw = setup.tile([P, CHUNKS, DH], BF16, name="w_raw%d" % g)
+        nc.sync.dma_start(out=raw[:], in_=w.rearrange("(c p) n -> p c n", p=P))
+        for h in range(PASSES):
+            rows = raw[:, h * PACK : (h + 1) * PACK, :]
+            cols = qk_grouped[:, h, g * 2 * DH : (g + 1) * 2 * DH, :]
+            nc.vector.tensor_copy(
+                out=cols.rearrange("p (r s c) j -> p r s c j", r=2, s=2)[:, :, 0, :, :],
+                in_=rows.rearrange("p j (r c) -> p r c j", r=2),
+            )
+            for e in range(2):
+                nc.vector.tensor_copy(
+                    out=cols.rearrange("p (r s i e) j -> p r s i e j", r=2, s=2, e=2)[
+                        :, :, 1, :, e, :
+                    ],
+                    in_=rows.rearrange("p j (r i e) -> p r i e j", r=2, e=2)[:, :, :, 1 - e, :],
+                )
+    raw = setup.tile([P, CHUNKS, DH], BF16, name="w_raw2")
+    nc.sync.dma_start(out=raw[:], in_=Wv.rearrange("(c p) n -> p c n", p=P))
+    for h in range(PASSES):
+        nc.vector.tensor_copy(
+            out=v_grouped[:, h, :, :],
+            in_=raw[:, h * PACK : (h + 1) * PACK, :].rearrange("p j n -> p n j"),
+        )
+
+    qk_codes = keep.tile([P, PASSES, BANK], U32, name="qk_codes", align_bytes=64)
+    qk_scales = keep.tile([P, PASSES, BANK], U8, name="qk_scales", align_bytes=64)
+    v_codes = keep.tile([P, PASSES, DH], U32, name="v_codes", align_bytes=64)
+    v_scales = keep.tile([P, PASSES, DH], U8, name="v_scales", align_bytes=64)
+    for h in range(PASSES):
+        nc.vector.quantize_mx(
+            out=qk_codes[:, h, :].bitcast(FP8X4),
+            scales=qk_scales[:, h, :],
+            in_=qk_grouped[:, h, :, :].rearrange("p c j -> p (c j)"),
+        )
+        nc.vector.quantize_mx(
+            out=v_codes[:, h, :].bitcast(FP8X4),
+            scales=v_scales[:, h, :],
+            in_=v_grouped[:, h, :, :].rearrange("p c j -> p (c j)"),
+        )
+    return qk_codes, qk_scales, v_codes, v_scales
+
+
+def build_rotary_table(nc, setup, keep):
+    ones = setup.tile([P, 1], F32, name="ones")
+    nc.vector.memset(ones[:], 1.0)
+    first_i = setup.tile([P, 1], I32, name="first_i")
+    nc.gpsimd.iota(first_i[:], pattern=[[0, 1]], base=0, channel_multiplier=TILES)
+    first = setup.tile([P, 1], F32, name="first")
+    nc.vector.tensor_copy(out=first[:], in_=first_i[:])
+
+    turns_hi = setup.tile([P, FREQS], F32, name="turns_hi")
+    turns_lo = setup.tile([P, FREQS], F32, name="turns_lo")
+    for c in range(FREQS):
+        sign = -1.0 if c % 2 == 0 else 1.0
+        turns = sign * 10000.0 ** (-c / FREQS) / (2.0 * math.pi)
+        hi = round(turns * HI_GRID) / HI_GRID
+        nc.gpsimd.memset(turns_hi[:, c : c + 1], hi)
+        nc.vector.tensor_scalar(
+            out=turns_lo[:, c : c + 1], in0=ones[:], scalar1=turns - hi, scalar2=None, op0=ALU.mult
+        )
+    turns_all = setup.tile([P, FREQS], F32, name="turns_all")
+    nc.vector.tensor_tensor(out=turns_all[:], in0=turns_hi[:], in1=turns_lo[:], op=ALU.add)
+
+    coarse = setup.tile([P, FREQS], F32, name="coarse")
+    nc.vector.tensor_scalar(
+        out=coarse[:], in0=turns_hi[:], scalar1=first[:, 0:1], scalar2=None, op0=ALU.mult
+    )
+    whole = setup.tile([P, FREQS], F32, name="whole")
+    nc.vector.tensor_scalar(
+        out=whole[:], in0=coarse[:], scalar1=ROUND_MAGIC, scalar2=ROUND_MAGIC,
+        op0=ALU.add, op1=ALU.subtract,
+    )
+    nc.vector.tensor_tensor(out=coarse[:], in0=coarse[:], in1=whole[:], op=ALU.subtract)
+
+    angle = setup.tile([P, TILES, FREQS], F32, name="angle")
+    nc.vector.scalar_tensor_tensor(
+        out=angle[:, 0, :], in0=turns_lo[:], scalar=first[:, 0:1], in1=coarse[:],
+        op0=ALU.mult, op1=ALU.add,
+    )
+    filled = 1
+    while filled < TILES:
+        nc.vector.scalar_tensor_tensor(
+            out=angle[:, filled : 2 * filled, :],
+            in0=turns_all[:].unsqueeze(1).to_broadcast([P, filled, FREQS]),
+            scalar=float(filled),
+            in1=angle[:, 0:filled, :],
+            op0=ALU.mult,
+            op1=ALU.add,
+        )
+        filled *= 2
+    scratch = setup.tile([P, TILES, FREQS], F32, name="scratch")
+    nc.vector.tensor_scalar(
+        out=scratch[:], in0=angle[:], scalar1=ROUND_MAGIC, scalar2=ROUND_MAGIC,
+        op0=ALU.add, op1=ALU.subtract,
+    )
+    nc.gpsimd.tensor_tensor(out=angle[:], in0=angle[:], in1=scratch[:], op=ALU.subtract)
+
+    table = keep.tile([P, TILES, 2, FREQS], F32, name="table")
+    nc.scalar.activation(out=table[:, :, 1, :], in_=angle[:], func=ACT.Sin, scale=2.0 * math.pi)
+    nc.scalar.activation(out=scratch[:], in_=angle[:], func=ACT.Sin, scale=math.pi)
+    nc.scalar.activation(out=scratch[:], in_=scratch[:], func=ACT.Square)
+    nc.gpsimd.tensor_scalar(
+        out=table[:, :, 0, :], in0=scratch[:], scalar1=-2.0, scalar2=1.0, op0=ALU.mult, op1=ALU.add
+    )
+    return table
+
+
+def tile_transformerlayershard_pa_t_kernel(
+    tc, x, ln_scale, ln_offset, Wq, Wk, Wv, out_0, out_1, out_2
+):
+    nc = tc.nc
+    x_rows = x.rearrange("b (p t) d -> p (b t) d", t=TILES)
+    q_rows = out_0.rearrange("(p t) h j -> p t (h j)", t=TILES)
+    k_rows = out_1.rearrange("(p t) h j -> p t (h j)", t=TILES)
+    v_rows = out_2.rearrange("(p t) h j -> p t (h j)", t=TILES)
+
+    with ExitStack() as ctx:
+        keep = ctx.enter_context(tc.tile_pool(name="keep", bufs=1))
+        setup = ctx.enter_context(tc.tile_pool(name="setup", bufs=1))
+        loads = ctx.enter_context(tc.tile_pool(name="loads", bufs=3))
+        work = ctx.enter_context(tc.tile_pool(name="work", bufs=2))
+        banks = ctx.enter_context(tc.psum_pool(name="banks", bufs=4))
+        qk_banks = ctx.enter_context(tc.psum_pool(name="qk_banks", bufs=3))
+        v_banks = ctx.enter_context(tc.psum_pool(name="v_banks", bufs=1))
+
+        ident = keep.tile([P, P], F32, name="ident")
+        make_identity(nc, ident[:])
+        gain_bias = load_layer_norm_columns(nc, setup, keep, banks, ident, ln_scale, ln_offset)
+        qk_codes, qk_scales, v_codes, v_scales = quantise_weights(nc, setup, keep, Wq, Wk, Wv)
+        table = build_rotary_table(nc, setup, keep)
+
+        for n in range(GROUPS):
+            tiles = slice(n * GROUP, (n + 1) * GROUP)
+            x_g = loads.tile([P, GROUP, D], BF16, tag="x_g")
+            nc.sync.dma_start(out=x_g[:], in_=x_rows[:, tiles, :])
+
+            sums = work.tile([P, GROUP], F32, tag="sums")
+            for t in range(GROUP):
+                unread_v = work.tile([P, D], BF16, tag="unread_v")
+                nc.vector.tensor_scalar(
+                    out=unread_v[:], in0=x_g[:, t, :], scalar1=1.0, scalar2=None,
+                    op0=ALU.mult, op1=ALU.add, accum_out=sums[:, t : t + 1],
+                )
+            neg_mean = work.tile([P, GROUP], F32, tag="neg_mean")
+            nc.vector.tensor_scalar(
+                out=neg_mean[:], in0=sums[:], scalar1=-1.0 / D, scalar2=None, op0=ALU.mult
+            )
+            squares = work.tile([P, GROUP], F32, tag="squares")
+            for t in range(GROUP):
+                unread_s = work.tile([P, D], BF16, tag="unread_s")
+                nc.scalar.activation(
+                    out=unread_s[:], in_=x_g[:, t, :], func=ACT.Square,
+                    bias=neg_mean[:, t : t + 1], scale=1.0, accum_out=squares[:, t : t + 1],
+                )
+            spread = work.tile([P, GROUP], F32, tag="spread")
+            nc.vector.tensor_scalar(
+                out=spread[:], in0=squares[:], scalar1=1.0 / D, scalar2=EPS,
+                op0=ALU.mult, op1=ALU.add,
+            )
+            nc.scalar.activation(out=spread[:], in_=spread[:], func=ACT.Sqrt)
+            rstd = work.tile([P, GROUP], F32, tag="rstd")
+            nc.vector.reciprocal(out=rstd[:], in_=spread[:])
+
+            y_g = work.tile([P, GROUP, D], F32, tag="y_g")
+            for t in range(GROUP):
+                engine = nc.vector if t % 2 == 0 else nc.gpsimd
+                engine.tensor_scalar(
+                    out=y_g[:, t, :], in0=x_g[:, t, :],
+                    scalar1=neg_mean[:, t : t + 1], scalar2=rstd[:, t : t + 1],
+                    op0=ALU.add, op1=ALU.mult,
+                )
+
+            planes = work.tile([P, CHUNKS, BANK], BF16, tag="planes")
+            for c in range(CHUNKS):
+                turned = banks.tile([P, BANK], F32, tag="turned")
+                for t in range(GROUP):
+                    nc.tensor.transpose(
+                        turned[:, t * P : (t + 1) * P], y_g[:, t, c * P : (c + 1) * P], ident[:]
+                    )
+                nc.scalar.activation(
+                    out=planes[:, c, :], in_=turned[:], func=ACT.Identity,
+                    scale=gain_bias[:, c : c + 1], bias=gain_bias[:, CHUNKS + c : CHUNKS + c + 1],
+                )
+
+            grouped = work.tile([P, PASSES, BANK, PACK], BF16, tag="grouped", align_bytes=64)
+            codes = work.tile([P, PASSES, BANK], U32, tag="codes", align_bytes=64)
+            scales = work.tile([P, PASSES, BANK], U8, tag="scales", align_bytes=64)
+            for h in range(PASSES):
+                nc.vector.tensor_copy(
+                    out=grouped[:, h, :, :].rearrange("p (w i) j -> p w j i", i=4),
+                    in_=planes[:, h * PACK : (h + 1) * PACK, :].rearrange(
+                        "p j (w i) -> p w j i", i=4
+                    ),
+                )
+            for h in range(PASSES):
+                nc.vector.quantize_mx(
+                    out=codes[:, h, :].bitcast(FP8X4),
+                    scales=scales[:, h, :],
+                    in_=grouped[:, h, :, :].rearrange("p w j -> p (w j)"),
+                )
+
+            products = work.tile([P, GROUP, 4, DH], F32, tag="products")
+            v_acc = v_banks.tile([P, BANK], F32, tag="v_acc")
+            for t in range(GROUP):
+                rows = slice(t * P, (t + 1) * P)
+                qk_acc = qk_banks.tile([P, BANK], F32, tag="qk_acc")
+                for h in range(PASSES):
+                    nc.tensor.matmul_mx(
+                        out=qk_acc[:],
+                        lhsT=codes[:, h, rows].bitcast(FP8X4),
+                        lhsT_scale=scales[:, h, rows],
+                        rhs=qk_codes[:, h, :].bitcast(FP8X4),
+                        rhs_scale=qk_scales[:, h, :],
+                        start=(h == 0),
+                        stop=(h == PASSES - 1),
+                    )
+                for h in range(PASSES):
+                    nc.tensor.matmul_mx(
+                        out=v_acc[:, rows],
+                        lhsT=codes[:, h, rows].bitcast(FP8X4),
+                        lhsT_scale=scales[:, h, rows],
+                        rhs=v_codes[:, h, :].bitcast(FP8X4),
+                        rhs_scale=v_scales[:, h, :],
+                        start=(h == 0),
+                        stop=(h == PASSES - 1),
+                    )
+                nc.vector.tensor_tensor(
+                    out=products[:, t, :, :],
+                    in0=qk_acc[:].rearrange("p (a w) -> p a w", a=4),
+                    in1=table[:, n * GROUP + t, :, :]
+                    .rearrange("p s c -> p (s c)")
+                    .unsqueeze(1)
+                    .to_broadcast([P, 4, DH]),
+                    op=ALU.mult,
+                )
+            v_out = work.tile([P, GROUP, DH], F32, tag="v_out")
+            nc.scalar.copy(out=v_out[:].rearrange("p t j -> p (t j)"), in_=v_acc[:])
+            qk_out = work.tile([P, GROUP, 2, DH], F32, tag="qk_out")
+            nc.gpsimd.tensor_tensor(
+                out=qk_out[:].rearrange("p t g (r c) -> p (t g r) c", r=2),
+                in0=products[:, :, :, 0:FREQS].rearrange("p t a c -> p (t a) c"),
+                in1=products[:, :, :, FREQS:DH].rearrange("p t a c -> p (t a) c"),
+                op=ALU.add,
+            )
+            nc.sync.dma_start(out=q_rows[:, tiles, :], in_=qk_out[:, :, 0, :])
+            nc.sync.dma_start(out=k_rows[:, tiles, :], in_=qk_out[:, :, 1, :])
+            nc.sync.dma_start(out=v_rows[:, tiles, :], in_=v_out[:])

@@ -217,8 +217,7 @@ def tile_transformerlayershard_pa_t_kernel(
 
             y_g = work.tile([P, GROUP, D], F32, tag="y_g")
             for t in range(GROUP):
-                engine = nc.vector if t % 2 == 0 else nc.gpsimd
-                engine.tensor_scalar(
+                nc.vector.tensor_scalar(
                     out=y_g[:, t, :], in0=x_g[:, t, :],
                     scalar1=neg_mean[:, t : t + 1], scalar2=rstd[:, t : t + 1],
                     op0=ALU.add, op1=ALU.mult,
@@ -290,7 +289,7 @@ def tile_transformerlayershard_pa_t_kernel(
             v_out = work.tile([P, GROUP, DH], F32, tag="v_out")
             nc.scalar.copy(out=v_out[:].rearrange("p t j -> p (t j)"), in_=v_acc[:])
             qk_out = work.tile([P, GROUP, 2, DH], F32, tag="qk_out")
-            nc.gpsimd.tensor_tensor(
+            nc.vector.tensor_tensor(
                 out=qk_out[:].rearrange("p t g (r c) -> p (t g r) c", r=2),
                 in0=products[:, :, :, 0:FREQS].rearrange("p t a c -> p (t a) c"),
                 in1=products[:, :, :, FREQS:DH].rearrange("p t a c -> p (t a) c"),

@@ -28,6 +28,7 @@ BANK = 512
 FREQS = DH // 2
 ROUND_MAGIC = 12582912.0
 HI_GRID = 2.0 ** 19
+TABLE_STEP = 16
 
 FLOPS = 2 * S * D * 3 * DH
 
@@ -94,27 +95,33 @@ def quantise_weights(nc, setup, keep, Wq, Wk, Wv):
     return qk_codes, qk_scales, v_codes, v_scales
 
 
-def build_rotary_table(nc, setup, keep):
-    ones = setup.tile([P, 1], F32, name="ones")
-    nc.vector.memset(ones[:], 1.0)
-    first_i = setup.tile([P, 1], I32, name="first_i")
-    nc.gpsimd.iota(first_i[:], pattern=[[0, 1]], base=0, channel_multiplier=TILES)
-    first = setup.tile([P, 1], F32, name="first")
-    nc.vector.tensor_copy(out=first[:], in_=first_i[:])
+def turns_per_position(c):
+    sign = -1.0 if c % 2 == 0 else 1.0
+    turns = sign * 10000.0 ** (-c / FREQS) / (2.0 * math.pi)
+    coarse = round(turns * HI_GRID) / HI_GRID
+    return coarse, turns - coarse
 
-    turns_hi = setup.tile([P, FREQS], F32, name="turns_hi")
+
+def fine_frequencies(nc, setup, one):
     turns_lo = setup.tile([P, FREQS], F32, name="turns_lo")
     for c in range(FREQS):
-        sign = -1.0 if c % 2 == 0 else 1.0
-        turns = sign * 10000.0 ** (-c / FREQS) / (2.0 * math.pi)
-        hi = round(turns * HI_GRID) / HI_GRID
-        nc.gpsimd.memset(turns_hi[:, c : c + 1], hi)
         nc.vector.tensor_scalar(
-            out=turns_lo[:, c : c + 1], in0=ones[:], scalar1=turns - hi, scalar2=None, op0=ALU.mult
+            out=turns_lo[:, c : c + 1], in0=one[:], scalar1=turns_per_position(c)[1],
+            scalar2=None, op0=ALU.mult,
         )
-    turns_all = setup.tile([P, FREQS], F32, name="turns_all")
-    nc.vector.tensor_tensor(out=turns_all[:], in0=turns_hi[:], in1=turns_lo[:], op=ALU.add)
+    return turns_lo
 
+
+def coarse_frequencies(nc, setup):
+    turns_hi = setup.tile([P, FREQS], F32, name="turns_hi")
+    for c in range(FREQS):
+        nc.vector.memset(turns_hi[:, c : c + 1], turns_per_position(c)[0])
+    return turns_hi
+
+
+def first_angles(nc, setup, first_i, turns_hi, turns_lo):
+    first = setup.tile([P, 1], F32, name="first")
+    nc.vector.tensor_copy(out=first[:], in_=first_i[:])
     coarse = setup.tile([P, FREQS], F32, name="coarse")
     nc.vector.tensor_scalar(
         out=coarse[:], in0=turns_hi[:], scalar1=first[:, 0:1], scalar2=None, op0=ALU.mult
@@ -125,12 +132,17 @@ def build_rotary_table(nc, setup, keep):
         op0=ALU.add, op1=ALU.subtract,
     )
     nc.vector.tensor_tensor(out=coarse[:], in0=coarse[:], in1=whole[:], op=ALU.subtract)
-
     angle = setup.tile([P, TILES, FREQS], F32, name="angle")
     nc.vector.scalar_tensor_tensor(
         out=angle[:, 0, :], in0=turns_lo[:], scalar=first[:, 0:1], in1=coarse[:],
         op0=ALU.mult, op1=ALU.add,
     )
+    return angle
+
+
+def all_angles(nc, setup, angle, turns_hi, turns_lo):
+    turns_all = setup.tile([P, FREQS], F32, name="turns_all")
+    nc.vector.tensor_tensor(out=turns_all[:], in0=turns_hi[:], in1=turns_lo[:], op=ALU.add)
     filled = 1
     while filled < TILES:
         nc.vector.scalar_tensor_tensor(
@@ -142,20 +154,31 @@ def build_rotary_table(nc, setup, keep):
             op1=ALU.add,
         )
         filled *= 2
-    scratch = setup.tile([P, TILES, FREQS], F32, name="scratch")
-    nc.vector.tensor_scalar(
-        out=scratch[:], in0=angle[:], scalar1=ROUND_MAGIC, scalar2=ROUND_MAGIC,
-        op0=ALU.add, op1=ALU.subtract,
-    )
-    nc.gpsimd.tensor_tensor(out=angle[:], in0=angle[:], in1=scratch[:], op=ALU.subtract)
+    for start in range(0, TILES, TABLE_STEP):
+        part = angle[:, start : start + TABLE_STEP, :]
+        whole_turns = setup.tile([P, TABLE_STEP, FREQS], F32, tag="whole_turns", bufs=2)
+        nc.vector.tensor_scalar(
+            out=whole_turns[:], in0=part, scalar1=ROUND_MAGIC, scalar2=ROUND_MAGIC,
+            op0=ALU.add, op1=ALU.subtract,
+        )
+        nc.gpsimd.tensor_tensor(out=part, in0=part, in1=whole_turns[:], op=ALU.subtract)
 
+
+def sines_and_cosines(nc, setup, keep, angle):
     table = keep.tile([P, TILES, 2, FREQS], F32, name="table")
-    nc.scalar.activation(out=table[:, :, 1, :], in_=angle[:], func=ACT.Sin, scale=2.0 * math.pi)
-    nc.scalar.activation(out=scratch[:], in_=angle[:], func=ACT.Sin, scale=math.pi)
-    nc.scalar.activation(out=scratch[:], in_=scratch[:], func=ACT.Square)
-    nc.gpsimd.tensor_scalar(
-        out=table[:, :, 0, :], in0=scratch[:], scalar1=-2.0, scalar2=1.0, op0=ALU.mult, op1=ALU.add
-    )
+    for start in range(0, TILES, TABLE_STEP):
+        part = angle[:, start : start + TABLE_STEP, :]
+        nc.scalar.activation(
+            out=table[:, start : start + TABLE_STEP, 1, :], in_=part, func=ACT.Sin,
+            scale=2.0 * math.pi,
+        )
+        half_sine = setup.tile([P, TABLE_STEP, FREQS], F32, tag="half_sine", bufs=2)
+        nc.scalar.activation(out=half_sine[:], in_=part, func=ACT.Sin, scale=math.pi)
+        nc.scalar.activation(out=half_sine[:], in_=half_sine[:], func=ACT.Square)
+        nc.gpsimd.tensor_scalar(
+            out=table[:, start : start + TABLE_STEP, 0, :], in0=half_sine[:],
+            scalar1=-2.0, scalar2=1.0, op0=ALU.mult, op1=ALU.add,
+        )
     return table
 
 
@@ -172,76 +195,88 @@ def tile_transformerlayershard_pa_t_kernel(
         keep = ctx.enter_context(tc.tile_pool(name="keep", bufs=1))
         setup = ctx.enter_context(tc.tile_pool(name="setup", bufs=1))
         loads = ctx.enter_context(tc.tile_pool(name="loads", bufs=3))
+        stats = ctx.enter_context(tc.tile_pool(name="stats", bufs=3))
         work = ctx.enter_context(tc.tile_pool(name="work", bufs=2))
-        banks = ctx.enter_context(tc.psum_pool(name="banks", bufs=4))
-        qk_banks = ctx.enter_context(tc.psum_pool(name="qk_banks", bufs=3))
+        banks = ctx.enter_context(tc.psum_pool(name="banks", bufs=3))
+        qk_banks = ctx.enter_context(tc.psum_pool(name="qk_banks", bufs=GROUP))
         v_banks = ctx.enter_context(tc.psum_pool(name="v_banks", bufs=1))
+        ctx.enter_context(tc.manual_schedule())
 
-        ident = keep.tile([P, P], F32, name="ident")
-        make_identity(nc, ident[:])
-        gain_bias = load_layer_norm_columns(nc, setup, keep, banks, ident, ln_scale, ln_offset)
-        qk_codes, qk_scales, v_codes, v_scales = quantise_weights(nc, setup, keep, Wq, Wk, Wv)
-        table = build_rotary_table(nc, setup, keep)
+        x_of, neg_mean_of, spread_of, y_of, planes_of = {}, {}, {}, {}, {}
+        codes_of, scales_of, qk_acc_of, v_acc_of = {}, {}, {}, {}
+        shared = {}
 
-        for n in range(GROUPS):
-            tiles = slice(n * GROUP, (n + 1) * GROUP)
+        def load(n):
             x_g = loads.tile([P, GROUP, D], BF16, tag="x_g")
-            nc.sync.dma_start(out=x_g[:], in_=x_rows[:, tiles, :])
+            nc.sync.dma_start(out=x_g[:], in_=x_rows[:, n * GROUP : (n + 1) * GROUP, :])
+            x_of[n] = x_g
 
-            sums = work.tile([P, GROUP], F32, tag="sums")
+        def row_sums(n):
+            sums = stats.tile([P, GROUP], F32, tag="sums")
             for t in range(GROUP):
                 unread_v = work.tile([P, D], BF16, tag="unread_v")
                 nc.vector.tensor_scalar(
-                    out=unread_v[:], in0=x_g[:, t, :], scalar1=1.0, scalar2=None,
+                    out=unread_v[:], in0=x_of[n][:, t, :], scalar1=1.0, scalar2=None,
                     op0=ALU.mult, op1=ALU.add, accum_out=sums[:, t : t + 1],
                 )
-            neg_mean = work.tile([P, GROUP], F32, tag="neg_mean")
+            neg_mean = stats.tile([P, GROUP], F32, tag="neg_mean")
             nc.vector.tensor_scalar(
                 out=neg_mean[:], in0=sums[:], scalar1=-1.0 / D, scalar2=None, op0=ALU.mult
             )
-            squares = work.tile([P, GROUP], F32, tag="squares")
+            neg_mean_of[n] = neg_mean
+
+        def row_spread(n):
+            squares = stats.tile([P, GROUP], F32, tag="squares")
             for t in range(GROUP):
                 unread_s = work.tile([P, D], BF16, tag="unread_s")
                 nc.scalar.activation(
-                    out=unread_s[:], in_=x_g[:, t, :], func=ACT.Square,
-                    bias=neg_mean[:, t : t + 1], scale=1.0, accum_out=squares[:, t : t + 1],
+                    out=unread_s[:], in_=x_of[n][:, t, :], func=ACT.Square,
+                    bias=neg_mean_of[n][:, t : t + 1], scale=1.0,
+                    accum_out=squares[:, t : t + 1],
                 )
-            spread = work.tile([P, GROUP], F32, tag="spread")
-            nc.vector.tensor_scalar(
-                out=spread[:], in0=squares[:], scalar1=1.0 / D, scalar2=EPS,
-                op0=ALU.mult, op1=ALU.add,
+            spread = stats.tile([P, GROUP], F32, tag="spread")
+            nc.scalar.activation(
+                out=spread[:], in_=squares[:], func=ACT.Sqrt, scale=1.0 / D,
+                bias=shared["eps"][:, 0:1],
             )
-            nc.scalar.activation(out=spread[:], in_=spread[:], func=ACT.Sqrt)
-            rstd = work.tile([P, GROUP], F32, tag="rstd")
-            nc.vector.reciprocal(out=rstd[:], in_=spread[:])
+            spread_of[n] = spread
 
+        def normalise(n):
+            rstd = stats.tile([P, GROUP], F32, tag="rstd")
+            nc.vector.reciprocal(out=rstd[:], in_=spread_of[n][:])
             y_g = work.tile([P, GROUP, D], F32, tag="y_g")
             for t in range(GROUP):
-                nc.vector.tensor_scalar(
-                    out=y_g[:, t, :], in0=x_g[:, t, :],
-                    scalar1=neg_mean[:, t : t + 1], scalar2=rstd[:, t : t + 1],
+                nc.gpsimd.tensor_scalar(
+                    out=y_g[:, t, :], in0=x_of[n][:, t, :],
+                    scalar1=neg_mean_of[n][:, t : t + 1], scalar2=rstd[:, t : t + 1],
                     op0=ALU.add, op1=ALU.mult,
                 )
+            y_of[n] = y_g
 
+        def turn(n):
+            gain_bias = shared["gain_bias"]
             planes = work.tile([P, CHUNKS, BANK], BF16, tag="planes")
             for c in range(CHUNKS):
                 turned = banks.tile([P, BANK], F32, tag="turned")
                 for t in range(GROUP):
                     nc.tensor.transpose(
-                        turned[:, t * P : (t + 1) * P], y_g[:, t, c * P : (c + 1) * P], ident[:]
+                        turned[:, t * P : (t + 1) * P], y_of[n][:, t, c * P : (c + 1) * P],
+                        shared["ident"][:],
                     )
                 nc.scalar.activation(
                     out=planes[:, c, :], in_=turned[:], func=ACT.Identity,
                     scale=gain_bias[:, c : c + 1], bias=gain_bias[:, CHUNKS + c : CHUNKS + c + 1],
                 )
+            planes_of[n] = planes
 
-            grouped = work.tile([P, PASSES, BANK, PACK], BF16, tag="grouped", align_bytes=64)
+        def pack(n):
+            grouped = work.tile([P, PASSES, BANK, PACK], BF16, tag="grouped", bufs=1, align_bytes=64)
             codes = work.tile([P, PASSES, BANK], U32, tag="codes", align_bytes=64)
             scales = work.tile([P, PASSES, BANK], U8, tag="scales", align_bytes=64)
             for h in range(PASSES):
                 nc.vector.tensor_copy(
                     out=grouped[:, h, :, :].rearrange("p (w i) j -> p w j i", i=4),
-                    in_=planes[:, h * PACK : (h + 1) * PACK, :].rearrange(
+                    in_=planes_of[n][:, h * PACK : (h + 1) * PACK, :].rearrange(
                         "p j (w i) -> p w j i", i=4
                     ),
                 )
@@ -251,9 +286,14 @@ def tile_transformerlayershard_pa_t_kernel(
                     scales=scales[:, h, :],
                     in_=grouped[:, h, :, :].rearrange("p w j -> p (w j)"),
                 )
+            codes_of[n] = codes
+            scales_of[n] = scales
 
-            products = work.tile([P, GROUP, 4, DH], F32, tag="products")
+        def project(n):
+            qk_codes, qk_scales, v_codes, v_scales = shared["weights"]
+            codes, scales = codes_of[n], scales_of[n]
             v_acc = v_banks.tile([P, BANK], F32, tag="v_acc")
+            qk_acc_of[n] = []
             for t in range(GROUP):
                 rows = slice(t * P, (t + 1) * P)
                 qk_acc = qk_banks.tile([P, BANK], F32, tag="qk_acc")
@@ -277,17 +317,22 @@ def tile_transformerlayershard_pa_t_kernel(
                         start=(h == 0),
                         stop=(h == PASSES - 1),
                     )
+                qk_acc_of[n].append(qk_acc)
+            v_acc_of[n] = v_acc
+
+        def rotate(n):
+            tiles = slice(n * GROUP, (n + 1) * GROUP)
+            products = work.tile([P, GROUP, 4, DH], F32, tag="products", bufs=1)
+            for t in range(GROUP):
                 nc.vector.tensor_tensor(
                     out=products[:, t, :, :],
-                    in0=qk_acc[:].rearrange("p (a w) -> p a w", a=4),
-                    in1=table[:, n * GROUP + t, :, :]
+                    in0=qk_acc_of[n][t][:].rearrange("p (a w) -> p a w", a=4),
+                    in1=shared["table"][:, n * GROUP + t, :, :]
                     .rearrange("p s c -> p (s c)")
                     .unsqueeze(1)
                     .to_broadcast([P, 4, DH]),
                     op=ALU.mult,
                 )
-            v_out = work.tile([P, GROUP, DH], F32, tag="v_out")
-            nc.scalar.copy(out=v_out[:].rearrange("p t j -> p (t j)"), in_=v_acc[:])
             qk_out = work.tile([P, GROUP, 2, DH], F32, tag="qk_out")
             nc.vector.tensor_tensor(
                 out=qk_out[:].rearrange("p t g (r c) -> p (t g r) c", r=2),
@@ -297,4 +342,51 @@ def tile_transformerlayershard_pa_t_kernel(
             )
             nc.sync.dma_start(out=q_rows[:, tiles, :], in_=qk_out[:, :, 0, :])
             nc.sync.dma_start(out=k_rows[:, tiles, :], in_=qk_out[:, :, 1, :])
+            v_out = work.tile([P, GROUP, DH], F32, tag="v_out")
+            nc.scalar.copy(out=v_out[:].rearrange("p t j -> p (t j)"), in_=v_acc_of[n][:])
             nc.sync.dma_start(out=v_rows[:, tiles, :], in_=v_out[:])
+
+        load(0)
+        ident = keep.tile([P, P], F32, name="ident")
+        make_identity(nc, ident[:])
+        shared["ident"] = ident
+        first_i = setup.tile([P, 1], I32, name="first_i")
+        nc.gpsimd.iota(first_i[:], pattern=[[0, 1]], base=0, channel_multiplier=TILES)
+        one = setup.tile([P, 1], F32, name="one")
+        nc.vector.memset(one[:], 1.0)
+        eps = keep.tile([P, 1], F32, name="eps")
+        nc.vector.tensor_scalar(out=eps[:], in0=one[:], scalar1=EPS, scalar2=None, op0=ALU.mult)
+        shared["eps"] = eps
+        turns_lo = fine_frequencies(nc, setup, one)
+        row_sums(0)
+        row_spread(0)
+        shared["gain_bias"] = load_layer_norm_columns(
+            nc, setup, keep, banks, ident, ln_scale, ln_offset
+        )
+        load(1)
+        load(2)
+        turns_hi = coarse_frequencies(nc, setup)
+        angle = first_angles(nc, setup, first_i, turns_hi, turns_lo)
+        normalise(0)
+        row_sums(1)
+        row_spread(1)
+        all_angles(nc, setup, angle, turns_hi, turns_lo)
+        turn(0)
+        shared["table"] = sines_and_cosines(nc, setup, keep, angle)
+        shared["weights"] = quantise_weights(nc, setup, keep, Wq, Wk, Wv)
+
+        for i in range(GROUPS + 1):
+            if i + 3 < GROUPS:
+                load(i + 3)
+            if i + 1 < GROUPS:
+                normalise(i + 1)
+            if i + 2 < GROUPS:
+                row_sums(i + 2)
+                row_spread(i + 2)
+            if i >= 1:
+                rotate(i - 1)
+            if i + 1 < GROUPS:
+                turn(i + 1)
+            if i < GROUPS:
+                pack(i)
+                project(i)

@@ -29,6 +29,7 @@ FREQS = DH // 2
 ROUND_MAGIC = 12582912.0
 HI_GRID = 2.0 ** 19
 TABLE_STEP = 16
+LOADS_AHEAD = 4
 
 FLOPS = 2 * S * D * 3 * DH
 
@@ -194,8 +195,8 @@ def tile_transformerlayershard_pa_t_kernel(
     with ExitStack() as ctx:
         keep = ctx.enter_context(tc.tile_pool(name="keep", bufs=1))
         setup = ctx.enter_context(tc.tile_pool(name="setup", bufs=1))
-        loads = ctx.enter_context(tc.tile_pool(name="loads", bufs=3))
-        stats = ctx.enter_context(tc.tile_pool(name="stats", bufs=3))
+        loads = ctx.enter_context(tc.tile_pool(name="loads", bufs=LOADS_AHEAD))
+        stats = ctx.enter_context(tc.tile_pool(name="stats", bufs=4))
         work = ctx.enter_context(tc.tile_pool(name="work", bufs=2))
         banks = ctx.enter_context(tc.psum_pool(name="banks", bufs=3))
         qk_banks = ctx.enter_context(tc.psum_pool(name="qk_banks", bufs=GROUP))
@@ -203,7 +204,7 @@ def tile_transformerlayershard_pa_t_kernel(
         ctx.enter_context(tc.manual_schedule())
 
         x_of, neg_mean_of, spread_of, y_of, planes_of = {}, {}, {}, {}, {}
-        codes_of, scales_of, qk_acc_of, v_acc_of = {}, {}, {}, {}
+        codes_of, scales_of, qk_acc_of, v_acc_of, products_of = {}, {}, {}, {}, {}
         shared = {}
 
         def load(n):
@@ -289,50 +290,53 @@ def tile_transformerlayershard_pa_t_kernel(
             codes_of[n] = codes
             scales_of[n] = scales
 
-        def project(n):
+        def project_tile(n, t):
             qk_codes, qk_scales, v_codes, v_scales = shared["weights"]
             codes, scales = codes_of[n], scales_of[n]
-            v_acc = v_banks.tile([P, BANK], F32, tag="v_acc")
-            qk_acc_of[n] = []
-            for t in range(GROUP):
-                rows = slice(t * P, (t + 1) * P)
-                qk_acc = qk_banks.tile([P, BANK], F32, tag="qk_acc")
-                for h in range(PASSES):
-                    nc.tensor.matmul_mx(
-                        out=qk_acc[:],
-                        lhsT=codes[:, h, rows].bitcast(FP8X4),
-                        lhsT_scale=scales[:, h, rows],
-                        rhs=qk_codes[:, h, :].bitcast(FP8X4),
-                        rhs_scale=qk_scales[:, h, :],
-                        start=(h == 0),
-                        stop=(h == PASSES - 1),
-                    )
-                for h in range(PASSES):
-                    nc.tensor.matmul_mx(
-                        out=v_acc[:, rows],
-                        lhsT=codes[:, h, rows].bitcast(FP8X4),
-                        lhsT_scale=scales[:, h, rows],
-                        rhs=v_codes[:, h, :].bitcast(FP8X4),
-                        rhs_scale=v_scales[:, h, :],
-                        start=(h == 0),
-                        stop=(h == PASSES - 1),
-                    )
-                qk_acc_of[n].append(qk_acc)
-            v_acc_of[n] = v_acc
-
-        def rotate(n):
-            tiles = slice(n * GROUP, (n + 1) * GROUP)
-            products = work.tile([P, GROUP, 4, DH], F32, tag="products", bufs=1)
-            for t in range(GROUP):
-                nc.vector.tensor_tensor(
-                    out=products[:, t, :, :],
-                    in0=qk_acc_of[n][t][:].rearrange("p (a w) -> p a w", a=4),
-                    in1=shared["table"][:, n * GROUP + t, :, :]
-                    .rearrange("p s c -> p (s c)")
-                    .unsqueeze(1)
-                    .to_broadcast([P, 4, DH]),
-                    op=ALU.mult,
+            rows = slice(t * P, (t + 1) * P)
+            if t == 0:
+                v_acc_of[n] = v_banks.tile([P, BANK], F32, tag="v_acc", name="v_acc")
+            qk_acc = qk_banks.tile([P, BANK], F32, tag="qk_acc")
+            for h in range(PASSES):
+                nc.tensor.matmul_mx(
+                    out=qk_acc[:],
+                    lhsT=codes[:, h, rows].bitcast(FP8X4),
+                    lhsT_scale=scales[:, h, rows],
+                    rhs=qk_codes[:, h, :].bitcast(FP8X4),
+                    rhs_scale=qk_scales[:, h, :],
+                    start=(h == 0),
+                    stop=(h == PASSES - 1),
                 )
+            for h in range(PASSES):
+                nc.tensor.matmul_mx(
+                    out=v_acc_of[n][:, rows],
+                    lhsT=codes[:, h, rows].bitcast(FP8X4),
+                    lhsT_scale=scales[:, h, rows],
+                    rhs=v_codes[:, h, :].bitcast(FP8X4),
+                    rhs_scale=v_scales[:, h, :],
+                    start=(h == 0),
+                    stop=(h == PASSES - 1),
+                )
+            qk_acc_of[(n, t)] = qk_acc
+
+        def rotate_tile(n, t):
+            if t == 0:
+                products_of[n] = work.tile(
+                    [P, GROUP, 4, DH], F32, tag="products", name="products", bufs=1
+                )
+            nc.vector.tensor_tensor(
+                out=products_of[n][:, t, :, :],
+                in0=qk_acc_of[(n, t)][:].rearrange("p (a w) -> p a w", a=4),
+                in1=shared["table"][:, n * GROUP + t, :, :]
+                .rearrange("p s c -> p (s c)")
+                .unsqueeze(1)
+                .to_broadcast([P, 4, DH]),
+                op=ALU.mult,
+            )
+
+        def store_qk(n):
+            tiles = slice(n * GROUP, (n + 1) * GROUP)
+            products = products_of[n]
             qk_out = work.tile([P, GROUP, 2, DH], F32, tag="qk_out")
             nc.vector.tensor_tensor(
                 out=qk_out[:].rearrange("p t g (r c) -> p (t g r) c", r=2),
@@ -342,11 +346,41 @@ def tile_transformerlayershard_pa_t_kernel(
             )
             nc.sync.dma_start(out=q_rows[:, tiles, :], in_=qk_out[:, :, 0, :])
             nc.sync.dma_start(out=k_rows[:, tiles, :], in_=qk_out[:, :, 1, :])
+
+        def store_v(n):
+            tiles = slice(n * GROUP, (n + 1) * GROUP)
             v_out = work.tile([P, GROUP, DH], F32, tag="v_out")
             nc.scalar.copy(out=v_out[:].rearrange("p t j -> p (t j)"), in_=v_acc_of[n][:])
             nc.sync.dma_start(out=v_rows[:, tiles, :], in_=v_out[:])
 
-        load(0)
+        def live(n):
+            return 0 <= n < GROUPS
+
+        def one_round(i):
+            if live(i + 5) and i + 5 >= LOADS_AHEAD:
+                load(i + 5)
+            if live(i - 1):
+                store_v(i - 1)
+            if live(i + 1):
+                turn(i + 1)
+            if live(i):
+                pack(i)
+            if live(i - 2):
+                store_qk(i - 2)
+            if live(i + 2):
+                normalise(i + 2)
+            for t in range(GROUP):
+                if live(i - 1):
+                    rotate_tile(i - 1, t)
+                if live(i):
+                    project_tile(i, t)
+            if live(i + 3):
+                row_spread(i + 3)
+            if live(i + 4):
+                row_sums(i + 4)
+
+        for n in range(LOADS_AHEAD):
+            load(n)
         ident = keep.tile([P, P], F32, name="ident")
         make_identity(nc, ident[:])
         shared["ident"] = ident
@@ -358,35 +392,18 @@ def tile_transformerlayershard_pa_t_kernel(
         nc.vector.tensor_scalar(out=eps[:], in0=one[:], scalar1=EPS, scalar2=None, op0=ALU.mult)
         shared["eps"] = eps
         turns_lo = fine_frequencies(nc, setup, one)
-        row_sums(0)
-        row_spread(0)
+        one_round(-4)
+        one_round(-3)
         shared["gain_bias"] = load_layer_norm_columns(
             nc, setup, keep, banks, ident, ln_scale, ln_offset
         )
-        load(1)
-        load(2)
         turns_hi = coarse_frequencies(nc, setup)
+        one_round(-2)
         angle = first_angles(nc, setup, first_i, turns_hi, turns_lo)
-        normalise(0)
-        row_sums(1)
-        row_spread(1)
+        one_round(-1)
         all_angles(nc, setup, angle, turns_hi, turns_lo)
-        turn(0)
-        shared["table"] = sines_and_cosines(nc, setup, keep, angle)
         shared["weights"] = quantise_weights(nc, setup, keep, Wq, Wk, Wv)
-
-        for i in range(GROUPS + 1):
-            if i + 3 < GROUPS:
-                load(i + 3)
-            if i + 1 < GROUPS:
-                normalise(i + 1)
-            if i + 2 < GROUPS:
-                row_sums(i + 2)
-                row_spread(i + 2)
-            if i >= 1:
-                rotate(i - 1)
-            if i + 1 < GROUPS:
-                turn(i + 1)
-            if i < GROUPS:
-                pack(i)
-                project(i)
+        one_round(0)
+        shared["table"] = sines_and_cosines(nc, setup, keep, angle)
+        for i in range(1, GROUPS + 2):
+            one_round(i)

@@ -22,9 +22,11 @@ PACK = 4
 CHUNKS = D // P
 PASSES = D // (P * PACK)
 TILES = S // P
-GROUP = 4
+GROUP = 2
 GROUPS = TILES // GROUP
 BANK = 512
+ROWS = GROUP * P
+PSUM_BANKS = 8
 FREQS = DH // 2
 ROUND_MAGIC = 12582912.0
 HI_GRID = 2.0 ** 19
@@ -175,7 +177,7 @@ def sines_and_cosines(nc, setup, keep, angle):
         )
         half_sine = setup.tile([P, TABLE_STEP, FREQS], F32, tag="half_sine", bufs=2)
         nc.scalar.activation(out=half_sine[:], in_=part, func=ACT.Sin, scale=math.pi)
-        nc.scalar.activation(out=half_sine[:], in_=half_sine[:], func=ACT.Square)
+        nc.vector.tensor_tensor(out=half_sine[:], in0=half_sine[:], in1=half_sine[:], op=ALU.mult)
         nc.gpsimd.tensor_scalar(
             out=table[:, start : start + TABLE_STEP, 0, :], in0=half_sine[:],
             scalar1=-2.0, scalar2=1.0, op0=ALU.mult, op1=ALU.add,
@@ -198,7 +200,7 @@ def tile_transformerlayershard_pa_t_kernel(
         loads = ctx.enter_context(tc.tile_pool(name="loads", bufs=LOADS_AHEAD))
         stats = ctx.enter_context(tc.tile_pool(name="stats", bufs=4))
         work = ctx.enter_context(tc.tile_pool(name="work", bufs=2))
-        banks = ctx.enter_context(tc.psum_pool(name="banks", bufs=3))
+        banks = ctx.enter_context(tc.psum_pool(name="banks", bufs=PSUM_BANKS - GROUP - 1))
         qk_banks = ctx.enter_context(tc.psum_pool(name="qk_banks", bufs=GROUP))
         v_banks = ctx.enter_context(tc.psum_pool(name="v_banks", bufs=1))
         ctx.enter_context(tc.manual_schedule())
@@ -256,9 +258,9 @@ def tile_transformerlayershard_pa_t_kernel(
 
         def turn(n):
             gain_bias = shared["gain_bias"]
-            planes = work.tile([P, CHUNKS, BANK], BF16, tag="planes")
+            planes = work.tile([P, CHUNKS, ROWS], BF16, tag="planes")
             for c in range(CHUNKS):
-                turned = banks.tile([P, BANK], F32, tag="turned")
+                turned = banks.tile([P, ROWS], F32, tag="turned")
                 for t in range(GROUP):
                     nc.tensor.transpose(
                         turned[:, t * P : (t + 1) * P], y_of[n][:, t, c * P : (c + 1) * P],
@@ -271,9 +273,9 @@ def tile_transformerlayershard_pa_t_kernel(
             planes_of[n] = planes
 
         def pack(n):
-            grouped = work.tile([P, PASSES, BANK, PACK], BF16, tag="grouped", bufs=1, align_bytes=64)
-            codes = work.tile([P, PASSES, BANK], U32, tag="codes", align_bytes=64)
-            scales = work.tile([P, PASSES, BANK], U8, tag="scales", align_bytes=64)
+            grouped = work.tile([P, PASSES, ROWS, PACK], BF16, tag="grouped", bufs=1, align_bytes=64)
+            codes = work.tile([P, PASSES, ROWS], U32, tag="codes", align_bytes=64)
+            scales = work.tile([P, PASSES, ROWS], U8, tag="scales", align_bytes=64)
             for h in range(PASSES):
                 nc.vector.tensor_copy(
                     out=grouped[:, h, :, :].rearrange("p (w i) j -> p w j i", i=4),
@@ -295,7 +297,7 @@ def tile_transformerlayershard_pa_t_kernel(
             codes, scales = codes_of[n], scales_of[n]
             rows = slice(t * P, (t + 1) * P)
             if t == 0:
-                v_acc_of[n] = v_banks.tile([P, BANK], F32, tag="v_acc", name="v_acc")
+                v_acc_of[n] = v_banks.tile([P, GROUP * DH], F32, tag="v_acc", name="v_acc")
             qk_acc = qk_banks.tile([P, BANK], F32, tag="qk_acc")
             for h in range(PASSES):
                 nc.tensor.matmul_mx(
@@ -350,7 +352,7 @@ def tile_transformerlayershard_pa_t_kernel(
         def store_v(n):
             tiles = slice(n * GROUP, (n + 1) * GROUP)
             v_out = work.tile([P, GROUP, DH], F32, tag="v_out")
-            nc.scalar.copy(out=v_out[:].rearrange("p t j -> p (t j)"), in_=v_acc_of[n][:])
+            nc.vector.tensor_copy(out=v_out[:].rearrange("p t j -> p (t j)"), in_=v_acc_of[n][:])
             nc.sync.dma_start(out=v_rows[:, tiles, :], in_=v_out[:])
 
         def live(n):
@@ -359,8 +361,6 @@ def tile_transformerlayershard_pa_t_kernel(
         def one_round(i):
             if live(i + 5) and i + 5 >= LOADS_AHEAD:
                 load(i + 5)
-            if live(i - 1):
-                store_v(i - 1)
             if live(i + 1):
                 turn(i + 1)
             if live(i):
@@ -369,6 +369,8 @@ def tile_transformerlayershard_pa_t_kernel(
                 store_qk(i - 2)
             if live(i + 2):
                 normalise(i + 2)
+            if live(i - 1):
+                store_v(i - 1)
             for t in range(GROUP):
                 if live(i - 1):
                     rotate_tile(i - 1, t)
@@ -397,8 +399,8 @@ def tile_transformerlayershard_pa_t_kernel(
         shared["gain_bias"] = load_layer_norm_columns(
             nc, setup, keep, banks, ident, ln_scale, ln_offset
         )
-        turns_hi = coarse_frequencies(nc, setup)
         one_round(-2)
+        turns_hi = coarse_frequencies(nc, setup)
         angle = first_angles(nc, setup, first_i, turns_hi, turns_lo)
         one_round(-1)
         all_angles(nc, setup, angle, turns_hi, turns_lo)

@@ -249,7 +249,8 @@ def tile_transformerlayershard_pa_t_kernel(
             nc.vector.reciprocal(out=rstd[:], in_=spread_of[n][:])
             y_g = work.tile([P, GROUP, D], F32, tag="y_g")
             for t in range(GROUP):
-                nc.gpsimd.tensor_scalar(
+                engine = nc.vector if t % 2 == 0 else nc.gpsimd
+                engine.tensor_scalar(
                     out=y_g[:, t, :], in0=x_of[n][:, t, :],
                     scalar1=neg_mean_of[n][:, t : t + 1], scalar2=rstd[:, t : t + 1],
                     op0=ALU.add, op1=ALU.mult,
@@ -352,7 +353,7 @@ def tile_transformerlayershard_pa_t_kernel(
         def store_v(n):
             tiles = slice(n * GROUP, (n + 1) * GROUP)
             v_out = work.tile([P, GROUP, DH], F32, tag="v_out")
-            nc.vector.tensor_copy(out=v_out[:].rearrange("p t j -> p (t j)"), in_=v_acc_of[n][:])
+            nc.scalar.copy(out=v_out[:].rearrange("p t j -> p (t j)"), in_=v_acc_of[n][:])
             nc.sync.dma_start(out=v_rows[:, tiles, :], in_=v_out[:])
 
         def live(n):

import math
from contextlib import ExitStack

import concourse.mybir as mybir
from concourse.masks import make_identity

F32 = mybir.dt.float32
BF16 = mybir.dt.bfloat16
I32 = mybir.dt.int32
U32 = mybir.dt.uint32
U8 = mybir.dt.uint8
FP8X4 = mybir.dt.float8_e4m3fn_x4
ALU = mybir.AluOpType
ACT = mybir.ActivationFunctionType

P = 128
S = 8192
D = 1024
DH = 128
EPS = 1e-5
PACK = 4
CHUNKS = D // P
PASSES = D // (P * PACK)
TILES = S // P
GROUP = 2
GROUPS = TILES // GROUP
BANK = 512
ROWS = GROUP * P
PSUM_BANKS = 8
FREQS = DH // 2
ROUND_MAGIC = 12582912.0
HI_GRID = 2.0 ** 19
TABLE_STEP = 16
LOADS_AHEAD = 4

FLOPS = 2 * S * D * 3 * DH


def load_layer_norm_columns(nc, setup, keep, banks, ident, ln_scale, ln_offset):
    rows = setup.tile([P, P], BF16, name="gb_rows")
    nc.vector.memset(rows[:], 0.0)
    nc.sync.dma_start(out=rows[0:CHUNKS, :], in_=ln_scale.rearrange("(c p) -> c p", p=P))
    nc.sync.dma_start(
        out=rows[CHUNKS : 2 * CHUNKS, :], in_=ln_offset.rearrange("(c p) -> c p", p=P)
    )
    rows32 = setup.tile([P, P], F32, name="gb_rows32")
    nc.vector.tensor_copy(out=rows32[:], in_=rows[:])
    turned = banks.tile([P, BANK], F32, tag="turned")
    nc.tensor.transpose(turned[:, 0:P], rows32[:], ident[:])
    gain_bias = keep.tile([P, 2 * CHUNKS], F32, name="gain_bias")
    nc.vector.tensor_copy(out=gain_bias[:], in_=turned[:, 0 : 2 * CHUNKS])
    return gain_bias


def quantise_weights(nc, setup, keep, Wq, Wk, Wv):
    qk_grouped = setup.tile([P, PASSES, BANK, PACK], BF16, name="qk_grouped", align_bytes=64)
    v_grouped = setup.tile([P, PASSES, DH, PACK], BF16, name="v_grouped", align_bytes=64)
    for g, w in enumerate((Wq, Wk)):
        raw = setup.tile([P, CHUNKS, DH], BF16, name="w_raw%d" % g)
        nc.sync.dma_start(out=raw[:], in_=w.rearrange("(c p) n -> p c n", p=P))
        for h in range(PASSES):
            rows = raw[:, h * PACK : (h + 1) * PACK, :]
            cols = qk_grouped[:, h, g * 2 * DH : (g + 1) * 2 * DH, :]
            nc.vector.tensor_copy(
                out=cols.rearrange("p (r s c) j -> p r s c j", r=2, s=2)[:, :, 0, :, :],
                in_=rows.rearrange("p j (r c) -> p r c j", r=2),
            )
            for e in range(2):
                nc.vector.tensor_copy(
                    out=cols.rearrange("p (r s i e) j -> p r s i e j", r=2, s=2, e=2)[
                        :, :, 1, :, e, :
                    ],
                    in_=rows.rearrange("p j (r i e) -> p r i e j", r=2, e=2)[:, :, :, 1 - e, :],
                )
    raw = setup.tile([P, CHUNKS, DH], BF16, name="w_raw2")
    nc.sync.dma_start(out=raw[:], in_=Wv.rearrange("(c p) n -> p c n", p=P))
    for h in range(PASSES):
        nc.vector.tensor_copy(
            out=v_grouped[:, h, :, :],
            in_=raw[:, h * PACK : (h + 1) * PACK, :].rearrange("p j n -> p n j"),
        )

    qk_codes = keep.tile([P, PASSES, BANK], U32, name="qk_codes", align_bytes=64)
    qk_scales = keep.tile([P, PASSES, BANK], U8, name="qk_scales", align_bytes=64)
    v_codes = keep.tile([P, PASSES, DH], U32, name="v_codes", align_bytes=64)
    v_scales = keep.tile([P, PASSES, DH], U8, name="v_scales", align_bytes=64)
    for h in range(PASSES):
        nc.vector.quantize_mx(
            out=qk_codes[:, h, :].bitcast(FP8X4),
            scales=qk_scales[:, h, :],
            in_=qk_grouped[:, h, :, :].rearrange("p c j -> p (c j)"),
        )
        nc.vector.quantize_mx(
            out=v_codes[:, h, :].bitcast(FP8X4),
            scales=v_scales[:, h, :],
            in_=v_grouped[:, h, :, :].rearrange("p c j -> p (c j)"),
        )
    return qk_codes, qk_scales, v_codes, v_scales


def turns_per_position(c):
    sign = -1.0 if c % 2 == 0 else 1.0
    turns = sign * 10000.0 ** (-c / FREQS) / (2.0 * math.pi)
    coarse = round(turns * HI_GRID) / HI_GRID
    return coarse, turns - coarse


def fine_frequencies(nc, setup, one):
    turns_lo = setup.tile([P, FREQS], F32, name="turns_lo")
    for c in range(FREQS):
        nc.vector.tensor_scalar(
            out=turns_lo[:, c : c + 1], in0=one[:], scalar1=turns_per_position(c)[1],
            scalar2=None, op0=ALU.mult,
        )
    return turns_lo


def coarse_frequencies(nc, setup):
    turns_hi = setup.tile([P, FREQS], F32, name="turns_hi")
    for c in range(FREQS):
        nc.vector.memset(turns_hi[:, c : c + 1], turns_per_position(c)[0])
    return turns_hi


def first_angles(nc, setup, first_i, turns_hi, turns_lo):
    first = setup.tile([P, 1], F32, name="first")
    nc.vector.tensor_copy(out=first[:], in_=first_i[:])
    coarse = setup.tile([P, FREQS], F32, name="coarse")
    nc.vector.tensor_scalar(
        out=coarse[:], in0=turns_hi[:], scalar1=first[:, 0:1], scalar2=None, op0=ALU.mult
    )
    whole = setup.tile([P, FREQS], F32, name="whole")
    nc.vector.tensor_scalar(
        out=whole[:], in0=coarse[:], scalar1=ROUND_MAGIC, scalar2=ROUND_MAGIC,
        op0=ALU.add, op1=ALU.subtract,
    )
    nc.vector.tensor_tensor(out=coarse[:], in0=coarse[:], in1=whole[:], op=ALU.subtract)
    angle = setup.tile([P, TILES, FREQS], F32, name="angle")
    nc.vector.scalar_tensor_tensor(
        out=angle[:, 0, :], in0=turns_lo[:], scalar=first[:, 0:1], in1=coarse[:],
        op0=ALU.mult, op1=ALU.add,
    )
    return angle


def all_angles(nc, setup, angle, turns_hi, turns_lo):
    turns_all = setup.tile([P, FREQS], F32, name="turns_all")
    nc.vector.tensor_tensor(out=turns_all[:], in0=turns_hi[:], in1=turns_lo[:], op=ALU.add)
    filled = 1
    while filled < TILES:
        nc.vector.scalar_tensor_tensor(
            out=angle[:, filled : 2 * filled, :],
            in0=turns_all[:].unsqueeze(1).to_broadcast([P, filled, FREQS]),
            scalar=float(filled),
            in1=angle[:, 0:filled, :],
            op0=ALU.mult,
            op1=ALU.add,
        )
        filled *= 2
    for start in range(0, TILES, TABLE_STEP):
        part = angle[:, start : start + TABLE_STEP, :]
        whole_turns = setup.tile([P, TABLE_STEP, FREQS], F32, tag="whole_turns", bufs=2)
        nc.vector.tensor_scalar(
            out=whole_turns[:], in0=part, scalar1=ROUND_MAGIC, scalar2=ROUND_MAGIC,
            op0=ALU.add, op1=ALU.subtract,
        )
        nc.gpsimd.tensor_tensor(out=part, in0=part, in1=whole_turns[:], op=ALU.subtract)


def sines_and_cosines(nc, setup, keep, angle):
    table = keep.tile([P, TILES, 2, FREQS], F32, name="table")
    for start in range(0, TILES, TABLE_STEP):
        part = angle[:, start : start + TABLE_STEP, :]
        nc.scalar.activation(
            out=table[:, start : start + TABLE_STEP, 1, :], in_=part, func=ACT.Sin,
            scale=2.0 * math.pi,
        )
        half_sine = setup.tile([P, TABLE_STEP, FREQS], F32, tag="half_sine", bufs=2)
        nc.scalar.activation(out=half_sine[:], in_=part, func=ACT.Sin, scale=math.pi)
        nc.vector.tensor_tensor(out=half_sine[:], in0=half_sine[:], in1=half_sine[:], op=ALU.mult)
        nc.gpsimd.tensor_scalar(
            out=table[:, start : start + TABLE_STEP, 0, :], in0=half_sine[:],
            scalar1=-2.0, scalar2=1.0, op0=ALU.mult, op1=ALU.add,
        )
    return table


def tile_transformerlayershard_pa_t_kernel(
    tc, x, ln_scale, ln_offset, Wq, Wk, Wv, out_0, out_1, out_2
):
    nc = tc.nc
    x_rows = x.rearrange("b (p t) d -> p (b t) d", t=TILES)
    q_rows = out_0.rearrange("(p t) h j -> p t (h j)", t=TILES)
    k_rows = out_1.rearrange("(p t) h j -> p t (h j)", t=TILES)
    v_rows = out_2.rearrange("(p t) h j -> p t (h j)", t=TILES)

    with ExitStack() as ctx:
        keep = ctx.enter_context(tc.tile_pool(name="keep", bufs=1))
        setup = ctx.enter_context(tc.tile_pool(name="setup", bufs=1))
        loads = ctx.enter_context(tc.tile_pool(name="loads", bufs=LOADS_AHEAD))
        stats = ctx.enter_context(tc.tile_pool(name="stats", bufs=4))
        work = ctx.enter_context(tc.tile_pool(name="work", bufs=2))
        banks = ctx.enter_context(tc.psum_pool(name="banks", bufs=PSUM_BANKS - GROUP - 1))
        qk_banks = ctx.enter_context(tc.psum_pool(name="qk_banks", bufs=GROUP))
        v_banks = ctx.enter_context(tc.psum_pool(name="v_banks", bufs=1))
        ctx.enter_context(tc.manual_schedule())

        x_of, neg_mean_of, spread_of, y_of, planes_of = {}, {}, {}, {}, {}
        codes_of, scales_of, qk_acc_of, v_acc_of, products_of = {}, {}, {}, {}, {}
        shared = {}

        def load(n):
            x_g = loads.tile([P, GROUP, D], BF16, tag="x_g")
            nc.sync.dma_start(out=x_g[:], in_=x_rows[:, n * GROUP : (n + 1) * GROUP, :])
            x_of[n] = x_g

        def row_sums(n):
            sums = stats.tile([P, GROUP], F32, tag="sums")
            for t in range(GROUP):
                unread_v = work.tile([P, D], BF16, tag="unread_v")
                nc.vector.tensor_scalar(
                    out=unread_v[:], in0=x_of[n][:, t, :], scalar1=1.0, scalar2=None,
                    op0=ALU.mult, op1=ALU.add, accum_out=sums[:, t : t + 1],
                )
            neg_mean = stats.tile([P, GROUP], F32, tag="neg_mean")
            nc.vector.tensor_scalar(
                out=neg_mean[:], in0=sums[:], scalar1=-1.0 / D, scalar2=None, op0=ALU.mult
            )
            neg_mean_of[n] = neg_mean

        def row_spread(n):
            squares = stats.tile([P, GROUP], F32, tag="squares")
            for t in range(GROUP):
                unread_s = work.tile([P, D], BF16, tag="unread_s")
                nc.scalar.activation(
                    out=unread_s[:], in_=x_of[n][:, t, :], func=ACT.Square,
                    bias=neg_mean_of[n][:, t : t + 1], scale=1.0,
                    accum_out=squares[:, t : t + 1],
                )
            spread = stats.tile([P, GROUP], F32, tag="spread")
            nc.scalar.activation(
                out=spread[:], in_=squares[:], func=ACT.Sqrt, scale=1.0 / D,
                bias=shared["eps"][:, 0:1],
            )
            spread_of[n] = spread

        def normalise(n):
            rstd = stats.tile([P, GROUP], F32, tag="rstd")
            nc.vector.reciprocal(out=rstd[:], in_=spread_of[n][:])
            y_g = work.tile([P, GROUP, D], F32, tag="y_g")
            for t in range(GROUP):
                engine = nc.vector if t % 2 == 0 else nc.gpsimd
                engine.tensor_scalar(
                    out=y_g[:, t, :], in0=x_of[n][:, t, :],
                    scalar1=neg_mean_of[n][:, t : t + 1], scalar2=rstd[:, t : t + 1],
                    op0=ALU.add, op1=ALU.mult,
                )
            y_of[n] = y_g

        def turn(n):
            gain_bias = shared["gain_bias"]
            planes = work.tile([P, CHUNKS, ROWS], BF16, tag="planes")
            for c in range(CHUNKS):
                turned = banks.tile([P, ROWS], F32, tag="turned")
                for t in range(GROUP):
                    nc.tensor.transpose(
                        turned[:, t * P : (t + 1) * P], y_of[n][:, t, c * P : (c + 1) * P],
                        shared["ident"][:],
                    )
                nc.scalar.activation(
                    out=planes[:, c, :], in_=turned[:], func=ACT.Identity,
                    scale=gain_bias[:, c : c + 1], bias=gain_bias[:, CHUNKS + c : CHUNKS + c + 1],
                )
            planes_of[n] = planes

        def pack(n):
            grouped = work.tile([P, PASSES, ROWS, PACK], BF16, tag="grouped", bufs=1, align_bytes=64)
            codes = work.tile([P, PASSES, ROWS], U32, tag="codes", align_bytes=64)
            scales = work.tile([P, PASSES, ROWS], U8, tag="scales", align_bytes=64)
            for h in range(PASSES):
                nc.vector.tensor_copy(
                    out=grouped[:, h, :, :].rearrange("p (w i) j -> p w j i", i=4),
                    in_=planes_of[n][:, h * PACK : (h + 1) * PACK, :].rearrange(
                        "p j (w i) -> p w j i", i=4
                    ),
                )
            for h in range(PASSES):
                nc.vector.quantize_mx(
                    out=codes[:, h, :].bitcast(FP8X4),
                    scales=scales[:, h, :],
                    in_=grouped[:, h, :, :].rearrange("p w j -> p (w j)"),
                )
            codes_of[n] = codes
            scales_of[n] = scales

        def project_tile(n, t):
            qk_codes, qk_scales, v_codes, v_scales = shared["weights"]
            codes, scales = codes_of[n], scales_of[n]
            rows = slice(t * P, (t + 1) * P)
            if t == 0:
                v_acc_of[n] = v_banks.tile([P, GROUP * DH], F32, tag="v_acc", name="v_acc")
            qk_acc = qk_banks.tile([P, BANK], F32, tag="qk_acc")
            for h in range(PASSES):
                nc.tensor.matmul_mx(
                    out=qk_acc[:],
                    lhsT=codes[:, h, rows].bitcast(FP8X4),
                    lhsT_scale=scales[:, h, rows],
                    rhs=qk_codes[:, h, :].bitcast(FP8X4),
                    rhs_scale=qk_scales[:, h, :],
                    start=(h == 0),
                    stop=(h == PASSES - 1),
                )
            for h in range(PASSES):
                nc.tensor.matmul_mx(
                    out=v_acc_of[n][:, rows],
                    lhsT=codes[:, h, rows].bitcast(FP8X4),
                    lhsT_scale=scales[:, h, rows],
                    rhs=v_codes[:, h, :].bitcast(FP8X4),
                    rhs_scale=v_scales[:, h, :],
                    start=(h == 0),
                    stop=(h == PASSES - 1),
                )
            qk_acc_of[(n, t)] = qk_acc

        def rotate_tile(n, t):
            if t == 0:
                products_of[n] = work.tile(
                    [P, GROUP, 4, DH], F32, tag="products", name="products", bufs=1
                )
            nc.vector.tensor_tensor(
                out=products_of[n][:, t, :, :],
                in0=qk_acc_of[(n, t)][:].rearrange("p (a w) -> p a w", a=4),
                in1=shared["table"][:, n * GROUP + t, :, :]
                .rearrange("p s c -> p (s c)")
                .unsqueeze(1)
                .to_broadcast([P, 4, DH]),
                op=ALU.mult,
            )

        def store_qk(n):
            tiles = slice(n * GROUP, (n + 1) * GROUP)
            products = products_of[n]
            qk_out = work.tile([P, GROUP, 2, DH], F32, tag="qk_out")
            nc.vector.tensor_tensor(
                out=qk_out[:].rearrange("p t g (r c) -> p (t g r) c", r=2),
                in0=products[:, :, :, 0:FREQS].rearrange("p t a c -> p (t a) c"),
                in1=products[:, :, :, FREQS:DH].rearrange("p t a c -> p (t a) c"),
                op=ALU.add,
            )
            nc.sync.dma_start(out=q_rows[:, tiles, :], in_=qk_out[:, :, 0, :])
            nc.sync.dma_start(out=k_rows[:, tiles, :], in_=qk_out[:, :, 1, :])

        def store_v(n):
            tiles = slice(n * GROUP, (n + 1) * GROUP)
            v_out = work.tile([P, GROUP, DH], F32, tag="v_out")
            nc.scalar.copy(out=v_out[:].rearrange("p t j -> p (t j)"), in_=v_acc_of[n][:])
            nc.sync.dma_start(out=v_rows[:, tiles, :], in_=v_out[:])

        def live(n):
            return 0 <= n < GROUPS

        def one_round(i):
            if live(i + 5) and i + 5 >= LOADS_AHEAD:
                load(i + 5)
            if live(i + 1):
                turn(i + 1)
            if live(i):
                pack(i)
            if live(i - 2):
                store_qk(i - 2)
            if live(i + 2):
                normalise(i + 2)
            if live(i - 1):
                store_v(i - 1)
            for t in range(GROUP):
                if live(i - 1):
                    rotate_tile(i - 1, t)
                if live(i):
                    project_tile(i, t)
            if live(i + 3):
                row_spread(i + 3)
            if live(i + 4):
                row_sums(i + 4)

        for n in range(LOADS_AHEAD):
            load(n)
        ident = keep.tile([P, P], F32, name="ident")
        make_identity(nc, ident[:])
        shared["ident"] = ident
        first_i = setup.tile([P, 1], I32, name="first_i")
        nc.gpsimd.iota(first_i[:], pattern=[[0, 1]], base=0, channel_multiplier=TILES)
        one = setup.tile([P, 1], F32, name="one")
        nc.vector.memset(one[:], 1.0)
        eps = keep.tile([P, 1], F32, name="eps")
        nc.vector.tensor_scalar(out=eps[:], in0=one[:], scalar1=EPS, scalar2=None, op0=ALU.mult)
        shared["eps"] = eps
        turns_lo = fine_frequencies(nc, setup, one)
        one_round(-4)
        one_round(-3)
        shared["gain_bias"] = load_layer_norm_columns(
            nc, setup, keep, banks, ident, ln_scale, ln_offset
        )
        one_round(-2)
        turns_hi = coarse_frequencies(nc, setup)
        angle = first_angles(nc, setup, first_i, turns_hi, turns_lo)
        one_round(-1)
        all_angles(nc, setup, angle, turns_hi, turns_lo)
        shared["weights"] = quantise_weights(nc, setup, keep, Wq, Wk, Wv)
        one_round(0)
        shared["table"] = sines_and_cosines(nc, setup, keep, angle)
        for i in range(1, GROUPS + 2):
            one_round(i)
